import numpy as np
import ml_dtypes

BF16 = ml_dtypes.bfloat16


def bf(x):
    return np.asarray(x, np.float32).astype(BF16)


def f32(x):
    return np.asarray(x, np.float32)


def f64(x):
    return np.asarray(x).astype(np.float64)


def striped(idx):
    return np.tile(idx.reshape(-1, 16).T, (8, 1))


H, H2, T, S, N = 128, 256, 384, 2048, 1024


def sigmoid(v):
    return 1.0 / (1.0 + np.exp(-v))


def setup_inputs():
    return {
        "base": f32(0.5 * np.random.standard_normal((H, S))),
        "ctx": bf(np.abs(np.random.standard_normal((H, N)))),
        "h": bf(np.abs(np.random.standard_normal((H, N)))),
        "wih": bf(np.random.standard_normal((H, T)) / np.sqrt(H)),
        "whh": bf(np.random.standard_normal((H, T)) / np.sqrt(H)),
        "bih": f32(0.3 * np.random.standard_normal((T, 1))),
        "bhh": f32(0.3 * np.random.standard_normal((T, 1))),
        "offs": striped(np.random.permutation(S)[:N]),
    }


def reference(base, ctx, h, wih, whh, bih, bhh, offs):
    idx = offs[:16].T.reshape(-1)
    ai = f64(wih).T @ f64(ctx) + f64(bih)
    ah = f64(whh).T @ f64(h) + f64(bhh)
    r = sigmoid(ai[:H] + ah[:H])
    z = sigmoid(ai[H:H2] + ah[H:H2])
    cand = np.tanh(ai[H2:] + r * ah[H2:])
    out = f64(base).copy()
    out[:, idx] = (1.0 - z) * cand + z * f64(h)
    return out

@@ -1,0 +1,92 @@
+import concourse.mybir as mybir
+
+F32 = mybir.dt.float32
+BF16 = mybir.dt.bfloat16
+U16 = mybir.dt.uint16
+ADD = mybir.AluOpType.add
+SUBTRACT = mybir.AluOpType.subtract
+MULT = mybir.AluOpType.mult
+SIGMOID = mybir.ActivationFunctionType.Sigmoid
+TANH = mybir.ActivationFunctionType.Tanh
+
+P = 128
+NODES = 1024
+STORE = 2048
+RESET, UPDATE, CAND = 0, 1, 2
+CHUNK = 512
+NCHUNKS = NODES // CHUNK
+
+FLOPS = 2 * 2 * P * 3 * P * NODES
+
+
+def gate_block(weights, gate):
+    return weights[:, gate * P : (gate + 1) * P]
+
+
+def tile_ampnn_kernel(tc, base, ctx, h, wih, whh, bih, bhh, offs, out):
+    nc = tc.nc
+    with tc.tile_pool(name="held", bufs=1) as held, tc.psum_pool(name="banks", bufs=1) as banks:
+        offsets = held.tile([P, NODES // 16], U16, name="offsets")
+        nc.sync.dma_start(offsets[:], offs)
+        wih_sb = held.tile([P, 3 * P], BF16, name="wih_sb")
+        nc.sync.dma_start(wih_sb[:], wih)
+        whh_sb = held.tile([P, 3 * P], BF16, name="whh_sb")
+        nc.scalar.dma_start(whh_sb[:], whh)
+        ctx_sb = held.tile([P, NODES], BF16, name="ctx_sb")
+        nc.sync.dma_start(ctx_sb[:], ctx)
+        h_sb = held.tile([P, NODES], BF16, name="h_sb")
+        nc.scalar.dma_start(h_sb[:], h)
+        bih_sb = held.tile([P, 3], F32, name="bih_sb")
+        bhh_sb = held.tile([P, 3], F32, name="bhh_sb")
+        with nc.allow_non_contiguous_dma(reason="384 biases, one float32 to a partition and gate"):
+            nc.gpsimd.dma_start(bih_sb[:], bih.rearrange("(g p) o -> p (g o)", p=P))
+            nc.gpsimd.dma_start(bhh_sb[:], bhh.rearrange("(g p) o -> p (g o)", p=P))
+        window = held.tile([P, STORE], F32, name="window")
+        nc.sync.dma_start(window[:], base)
+
+        bias_rz = held.tile([P, 2], F32, name="bias_rz")
+        nc.vector.tensor_tensor(bias_rz[:], bih_sb[:, RESET : UPDATE + 1], bhh_sb[:, RESET : UPDATE + 1], ADD)
+        neg_bih_cand = held.tile([P, 1], F32, name="neg_bih_cand")
+        nc.vector.tensor_scalar_mul(neg_bih_cand[:], bih_sb[:, CAND : CAND + 1], -1.0)
+
+        chunks = [slice(c * CHUNK, (c + 1) * CHUNK) for c in range(NCHUNKS)]
+
+        tanh_args = []
+        for c, cols in enumerate(chunks):
+            acc_r = banks.tile([P, CHUNK], F32, name=f"acc_r{c}")
+            nc.tensor.matmul(acc_r[:], gate_block(wih_sb, RESET), ctx_sb[:, cols], start=True, stop=False)
+            nc.tensor.matmul(acc_r[:], gate_block(whh_sb, RESET), h_sb[:, cols], start=False, stop=True)
+            acc_hc = banks.tile([P, CHUNK], F32, name=f"acc_hc{c}")
+            nc.tensor.matmul(acc_hc[:], gate_block(whh_sb, CAND), h_sb[:, cols], start=True, stop=True)
+            acc_ic = banks.tile([P, CHUNK], F32, name=f"acc_ic{c}")
+            nc.tensor.matmul(acc_ic[:], gate_block(wih_sb, CAND), ctx_sb[:, cols], start=True, stop=True)
+
+            r = held.tile([P, CHUNK], F32, name=f"r{c}")
+            nc.scalar.activation(r[:], acc_r[:], SIGMOID, bias=bias_rz[:, RESET : RESET + 1])
+            gated = held.tile([P, CHUNK], F32, name=f"gated{c}")
+            nc.vector.scalar_tensor_tensor(
+                gated[:], acc_hc[:], bhh_sb[:, CAND : CAND + 1], r[:], op0=ADD, op1=MULT
+            )
+            tanh_arg = held.tile([P, CHUNK], F32, name=f"tanh_arg{c}")
+            nc.vector.tensor_tensor(tanh_arg[:], gated[:], acc_ic[:], ADD)
+            tanh_args.append(tanh_arg)
+
+        kept = held.tile([P, NODES], F32, name="kept")
+        zs = []
+        for c, cols in enumerate(chunks):
+            acc_z = banks.tile([P, CHUNK], F32, name=f"acc_z{c}")
+            nc.tensor.matmul(acc_z[:], gate_block(wih_sb, UPDATE), ctx_sb[:, cols], start=True, stop=False)
+            nc.tensor.matmul(acc_z[:], gate_block(whh_sb, UPDATE), h_sb[:, cols], start=False, stop=True)
+            z = held.tile([P, CHUNK], F32, name=f"z{c}")
+            nc.scalar.activation(z[:], acc_z[:], SIGMOID, bias=bias_rz[:, UPDATE : UPDATE + 1])
+            nc.gpsimd.tensor_tensor(kept[:, cols], z[:], h_sb[:, cols], MULT)
+            zs.append(z)
+
+        fresh = held.tile([P, NODES], F32, name="fresh")
+        for c, cols in enumerate(chunks):
+            neg_cand = held.tile([P, CHUNK], F32, name=f"neg_cand{c}")
+            nc.scalar.activation(neg_cand[:], tanh_args[c][:], TANH, bias=neg_bih_cand[:], scale=-1.0)
+            nc.vector.scalar_tensor_tensor(fresh[:, cols], zs[c][:], 1.0, neg_cand[:], op0=SUBTRACT, op1=MULT)
+
+        nc.vector.tensor_tensor(window[:].indirect(offsets[:]), fresh[:], kept[:], ADD)
+        nc.sync.dma_start(out, window[:])

@@ -26,8 +26,6 @@ def gate_block(weights, gate):
 def tile_ampnn_kernel(tc, base, ctx, h, wih, whh, bih, bhh, offs, out):
     nc = tc.nc
     with tc.tile_pool(name="held", bufs=1) as held, tc.psum_pool(name="banks", bufs=1) as banks:
-        offsets = held.tile([P, NODES // 16], U16, name="offsets")
-        nc.sync.dma_start(offsets[:], offs)
         wih_sb = held.tile([P, 3 * P], BF16, name="wih_sb")
         nc.sync.dma_start(wih_sb[:], wih)
         whh_sb = held.tile([P, 3 * P], BF16, name="whh_sb")
@@ -39,10 +37,16 @@ def tile_ampnn_kernel(tc, base, ctx, h, wih, whh, bih, bhh, offs, out):
         bih_sb = held.tile([P, 3], F32, name="bih_sb")
         bhh_sb = held.tile([P, 3], F32, name="bhh_sb")
         with nc.allow_non_contiguous_dma(reason="384 biases, one float32 to a partition and gate"):
-            nc.gpsimd.dma_start(bih_sb[:], bih.rearrange("(g p) o -> p (g o)", p=P))
-            nc.gpsimd.dma_start(bhh_sb[:], bhh.rearrange("(g p) o -> p (g o)", p=P))
+            nc.sync.dma_start(bih_sb[:], bih.rearrange("(g p) o -> p (g o)", p=P))
+            nc.scalar.dma_start(bhh_sb[:], bhh.rearrange("(g p) o -> p (g o)", p=P))
+        offsets = held.tile([P, NODES // 16], U16, name="offsets")
+        nc.sync.dma_start(offsets[:], offs)
         window = held.tile([P, STORE], F32, name="window")
         nc.sync.dma_start(window[:], base)
+
+        table_warmer = held.tile([P, 1], F32, name="table_warmer")
+        nc.vector.memset(table_warmer[:], 0.0)
+        nc.scalar.activation(table_warmer[:], table_warmer[:], SIGMOID)
 
         bias_rz = held.tile([P, 2], F32, name="bias_rz")
         nc.vector.tensor_tensor(bias_rz[:], bih_sb[:, RESET : UPDATE + 1], bhh_sb[:, RESET : UPDATE + 1], ADD)

@@ -15,6 +15,8 @@ STORE = 2048
 RESET, UPDATE, CAND = 0, 1, 2
 CHUNK = 512
 NCHUNKS = NODES // CHUNK
+PSUM_BANKS = 8
+WARMUP_MATMULS = 5
 
 FLOPS = 2 * 2 * P * 3 * P * NODES
 
@@ -25,7 +27,7 @@ def gate_block(weights, gate):
 
 def tile_ampnn_kernel(tc, base, ctx, h, wih, whh, bih, bhh, offs, out):
     nc = tc.nc
-    with tc.tile_pool(name="held", bufs=1) as held, tc.psum_pool(name="banks", bufs=1) as banks:
+    with tc.tile_pool(name="held", bufs=1) as held, tc.psum_pool(name="banks", bufs=PSUM_BANKS) as banks:
         wih_sb = held.tile([P, 3 * P], BF16, name="wih_sb")
         nc.sync.dma_start(wih_sb[:], wih)
         whh_sb = held.tile([P, 3 * P], BF16, name="whh_sb")
@@ -48,6 +50,12 @@ def tile_ampnn_kernel(tc, base, ctx, h, wih, whh, bih, bhh, offs, out):
         nc.vector.memset(table_warmer[:], 0.0)
         nc.scalar.activation(table_warmer[:], table_warmer[:], SIGMOID)
 
+        zeros = held.tile([P, CHUNK], BF16, name="zeros")
+        nc.vector.memset(zeros[:], 0.0)
+        unread = banks.tile([P, CHUNK], F32, tag="bank", name="unread")
+        for repeat in range(WARMUP_MATMULS):
+            nc.tensor.matmul(unread[:], zeros[:, 0:P], zeros[:], start=True, stop=True)
+
         bias_rz = held.tile([P, 2], F32, name="bias_rz")
         nc.vector.tensor_tensor(bias_rz[:], bih_sb[:, RESET : UPDATE + 1], bhh_sb[:, RESET : UPDATE + 1], ADD)
         neg_bih_cand = held.tile([P, 1], F32, name="neg_bih_cand")
@@ -57,12 +65,12 @@ def tile_ampnn_kernel(tc, base, ctx, h, wih, whh, bih, bhh, offs, out):
 
         tanh_args = []
         for c, cols in enumerate(chunks):
-            acc_r = banks.tile([P, CHUNK], F32, name=f"acc_r{c}")
+            acc_r = banks.tile([P, CHUNK], F32, tag="bank", name=f"acc_r{c}")
             nc.tensor.matmul(acc_r[:], gate_block(wih_sb, RESET), ctx_sb[:, cols], start=True, stop=False)
             nc.tensor.matmul(acc_r[:], gate_block(whh_sb, RESET), h_sb[:, cols], start=False, stop=True)
-            acc_hc = banks.tile([P, CHUNK], F32, name=f"acc_hc{c}")
+            acc_hc = banks.tile([P, CHUNK], F32, tag="bank", name=f"acc_hc{c}")
             nc.tensor.matmul(acc_hc[:], gate_block(whh_sb, CAND), h_sb[:, cols], start=True, stop=True)
-            acc_ic = banks.tile([P, CHUNK], F32, name=f"acc_ic{c}")
+            acc_ic = banks.tile([P, CHUNK], F32, tag="bank", name=f"acc_ic{c}")
             nc.tensor.matmul(acc_ic[:], gate_block(wih_sb, CAND), ctx_sb[:, cols], start=True, stop=True)
 
             r = held.tile([P, CHUNK], F32, name=f"r{c}")
@@ -78,7 +86,7 @@ def tile_ampnn_kernel(tc, base, ctx, h, wih, whh, bih, bhh, offs, out):
         kept = held.tile([P, NODES], F32, name="kept")
         zs = []
         for c, cols in enumerate(chunks):
-            acc_z = banks.tile([P, CHUNK], F32, name=f"acc_z{c}")
+            acc_z = banks.tile([P, CHUNK], F32, tag="bank", name=f"acc_z{c}")
             nc.tensor.matmul(acc_z[:], gate_block(wih_sb, UPDATE), ctx_sb[:, cols], start=True, stop=False)
             nc.tensor.matmul(acc_z[:], gate_block(whh_sb, UPDATE), h_sb[:, cols], start=False, stop=True)
             z = held.tile([P, CHUNK], F32, name=f"z{c}")

@@ -16,7 +16,7 @@ RESET, UPDATE, CAND = 0, 1, 2
 CHUNK = 512
 NCHUNKS = NODES // CHUNK
 PSUM_BANKS = 8
-WARMUP_MATMULS = 5
+WARMUP_MATMULS = 3
 
 FLOPS = 2 * 2 * P * 3 * P * NODES
 
@@ -27,15 +27,23 @@ def gate_block(weights, gate):
 
 def tile_ampnn_kernel(tc, base, ctx, h, wih, whh, bih, bhh, offs, out):
     nc = tc.nc
+    chunks = [slice(c * CHUNK, (c + 1) * CHUNK) for c in range(NCHUNKS)]
     with tc.tile_pool(name="held", bufs=1) as held, tc.psum_pool(name="banks", bufs=PSUM_BANKS) as banks:
+        zeros = held.tile([P, CHUNK], BF16, name="zeros")
+        nc.gpsimd.memset(zeros[:], 0.0)
+        unread = banks.tile([P, CHUNK], F32, tag="bank", name="unread")
+        for repeat in range(WARMUP_MATMULS):
+            nc.tensor.matmul(unread[:], zeros[:, 0:P], zeros[:], start=True, stop=True)
+
         wih_sb = held.tile([P, 3 * P], BF16, name="wih_sb")
         nc.sync.dma_start(wih_sb[:], wih)
         whh_sb = held.tile([P, 3 * P], BF16, name="whh_sb")
         nc.scalar.dma_start(whh_sb[:], whh)
         ctx_sb = held.tile([P, NODES], BF16, name="ctx_sb")
-        nc.sync.dma_start(ctx_sb[:], ctx)
         h_sb = held.tile([P, NODES], BF16, name="h_sb")
-        nc.scalar.dma_start(h_sb[:], h)
+        for cols in chunks:
+            nc.sync.dma_start(ctx_sb[:, cols], ctx[:, cols])
+            nc.scalar.dma_start(h_sb[:, cols], h[:, cols])
         bih_sb = held.tile([P, 3], F32, name="bih_sb")
         bhh_sb = held.tile([P, 3], F32, name="bhh_sb")
         with nc.allow_non_contiguous_dma(reason="384 biases, one float32 to a partition and gate"):
@@ -50,55 +58,54 @@ def tile_ampnn_kernel(tc, base, ctx, h, wih, whh, bih, bhh, offs, out):
         nc.vector.memset(table_warmer[:], 0.0)
         nc.scalar.activation(table_warmer[:], table_warmer[:], SIGMOID)
 
-        zeros = held.tile([P, CHUNK], BF16, name="zeros")
-        nc.vector.memset(zeros[:], 0.0)
-        unread = banks.tile([P, CHUNK], F32, tag="bank", name="unread")
-        for repeat in range(WARMUP_MATMULS):
-            nc.tensor.matmul(unread[:], zeros[:, 0:P], zeros[:], start=True, stop=True)
-
         bias_rz = held.tile([P, 2], F32, name="bias_rz")
         nc.vector.tensor_tensor(bias_rz[:], bih_sb[:, RESET : UPDATE + 1], bhh_sb[:, RESET : UPDATE + 1], ADD)
         neg_bih_cand = held.tile([P, 1], F32, name="neg_bih_cand")
         nc.vector.tensor_scalar_mul(neg_bih_cand[:], bih_sb[:, CAND : CAND + 1], -1.0)
 
-        chunks = [slice(c * CHUNK, (c + 1) * CHUNK) for c in range(NCHUNKS)]
+        r = [held.tile([P, CHUNK], F32, name=f"r{c}") for c in range(NCHUNKS)]
+        z = [held.tile([P, CHUNK], F32, name=f"z{c}") for c in range(NCHUNKS)]
+        tanh_arg = [held.tile([P, CHUNK], F32, name=f"tanh_arg{c}") for c in range(NCHUNKS)]
+        kept = held.tile([P, NODES], F32, name="kept")
+        fresh = held.tile([P, NODES], F32, name="fresh")
 
-        tanh_args = []
-        for c, cols in enumerate(chunks):
+        def reset_gate(c):
             acc_r = banks.tile([P, CHUNK], F32, tag="bank", name=f"acc_r{c}")
-            nc.tensor.matmul(acc_r[:], gate_block(wih_sb, RESET), ctx_sb[:, cols], start=True, stop=False)
-            nc.tensor.matmul(acc_r[:], gate_block(whh_sb, RESET), h_sb[:, cols], start=False, stop=True)
-            acc_hc = banks.tile([P, CHUNK], F32, tag="bank", name=f"acc_hc{c}")
-            nc.tensor.matmul(acc_hc[:], gate_block(whh_sb, CAND), h_sb[:, cols], start=True, stop=True)
-            acc_ic = banks.tile([P, CHUNK], F32, tag="bank", name=f"acc_ic{c}")
-            nc.tensor.matmul(acc_ic[:], gate_block(wih_sb, CAND), ctx_sb[:, cols], start=True, stop=True)
+            nc.tensor.matmul(acc_r[:], gate_block(wih_sb, RESET), ctx_sb[:, chunks[c]], start=True, stop=False)
+            nc.tensor.matmul(acc_r[:], gate_block(whh_sb, RESET), h_sb[:, chunks[c]], start=False, stop=True)
+            nc.scalar.activation(r[c][:], acc_r[:], SIGMOID, bias=bias_rz[:, RESET : RESET + 1])
 
-            r = held.tile([P, CHUNK], F32, name=f"r{c}")
-            nc.scalar.activation(r[:], acc_r[:], SIGMOID, bias=bias_rz[:, RESET : RESET + 1])
+        def tanh_argument(c):
+            acc_hc = banks.tile([P, CHUNK], F32, tag="bank", name=f"acc_hc{c}")
+            nc.tensor.matmul(acc_hc[:], gate_block(whh_sb, CAND), h_sb[:, chunks[c]], start=True, stop=True)
+            acc_ic = banks.tile([P, CHUNK], F32, tag="bank", name=f"acc_ic{c}")
+            nc.tensor.matmul(acc_ic[:], gate_block(wih_sb, CAND), ctx_sb[:, chunks[c]], start=True, stop=True)
             gated = held.tile([P, CHUNK], F32, name=f"gated{c}")
             nc.vector.scalar_tensor_tensor(
-                gated[:], acc_hc[:], bhh_sb[:, CAND : CAND + 1], r[:], op0=ADD, op1=MULT
+                gated[:], acc_hc[:], bhh_sb[:, CAND : CAND + 1], r[c][:], op0=ADD, op1=MULT
             )
-            tanh_arg = held.tile([P, CHUNK], F32, name=f"tanh_arg{c}")
-            nc.vector.tensor_tensor(tanh_arg[:], gated[:], acc_ic[:], ADD)
-            tanh_args.append(tanh_arg)
+            nc.vector.tensor_tensor(tanh_arg[c][:], gated[:], acc_ic[:], ADD)
 
-        kept = held.tile([P, NODES], F32, name="kept")
-        zs = []
-        for c, cols in enumerate(chunks):
+        def update_gate(c, engine):
             acc_z = banks.tile([P, CHUNK], F32, tag="bank", name=f"acc_z{c}")
-            nc.tensor.matmul(acc_z[:], gate_block(wih_sb, UPDATE), ctx_sb[:, cols], start=True, stop=False)
-            nc.tensor.matmul(acc_z[:], gate_block(whh_sb, UPDATE), h_sb[:, cols], start=False, stop=True)
-            z = held.tile([P, CHUNK], F32, name=f"z{c}")
-            nc.scalar.activation(z[:], acc_z[:], SIGMOID, bias=bias_rz[:, UPDATE : UPDATE + 1])
-            nc.gpsimd.tensor_tensor(kept[:, cols], z[:], h_sb[:, cols], MULT)
-            zs.append(z)
+            nc.tensor.matmul(acc_z[:], gate_block(wih_sb, UPDATE), ctx_sb[:, chunks[c]], start=True, stop=False)
+            nc.tensor.matmul(acc_z[:], gate_block(whh_sb, UPDATE), h_sb[:, chunks[c]], start=False, stop=True)
+            nc.scalar.activation(z[c][:], acc_z[:], SIGMOID, bias=bias_rz[:, UPDATE : UPDATE + 1])
+            engine.tensor_tensor(kept[:, chunks[c]], z[c][:], h_sb[:, chunks[c]], MULT)
 
-        fresh = held.tile([P, NODES], F32, name="fresh")
-        for c, cols in enumerate(chunks):
+        def candidate(c):
             neg_cand = held.tile([P, CHUNK], F32, name=f"neg_cand{c}")
-            nc.scalar.activation(neg_cand[:], tanh_args[c][:], TANH, bias=neg_bih_cand[:], scale=-1.0)
-            nc.vector.scalar_tensor_tensor(fresh[:, cols], zs[c][:], 1.0, neg_cand[:], op0=SUBTRACT, op1=MULT)
+            nc.scalar.activation(neg_cand[:], tanh_arg[c][:], TANH, bias=neg_bih_cand[:], scale=-1.0)
+            nc.vector.scalar_tensor_tensor(fresh[:, chunks[c]], z[c][:], 1.0, neg_cand[:], op0=SUBTRACT, op1=MULT)
+
+        reset_gate(0)
+        tanh_argument(0)
+        reset_gate(1)
+        update_gate(0, nc.gpsimd)
+        tanh_argument(1)
+        candidate(0)
+        update_gate(1, nc.vector)
+        candidate(1)
 
         nc.vector.tensor_tensor(window[:].indirect(offsets[:]), fresh[:], kept[:], ADD)
         nc.sync.dma_start(out, window[:])

@@ -63,49 +63,50 @@ def tile_ampnn_kernel(tc, base, ctx, h, wih, whh, bih, bhh, offs, out):
         neg_bih_cand = held.tile([P, 1], F32, name="neg_bih_cand")
         nc.vector.tensor_scalar_mul(neg_bih_cand[:], bih_sb[:, CAND : CAND + 1], -1.0)
 
-        r = [held.tile([P, CHUNK], F32, name=f"r{c}") for c in range(NCHUNKS)]
-        z = [held.tile([P, CHUNK], F32, name=f"z{c}") for c in range(NCHUNKS)]
-        tanh_arg = [held.tile([P, CHUNK], F32, name=f"tanh_arg{c}") for c in range(NCHUNKS)]
         kept = held.tile([P, NODES], F32, name="kept")
         fresh = held.tile([P, NODES], F32, name="fresh")
 
-        def reset_gate(c):
-            acc_r = banks.tile([P, CHUNK], F32, tag="bank", name=f"acc_r{c}")
-            nc.tensor.matmul(acc_r[:], gate_block(wih_sb, RESET), ctx_sb[:, chunks[c]], start=True, stop=False)
-            nc.tensor.matmul(acc_r[:], gate_block(whh_sb, RESET), h_sb[:, chunks[c]], start=False, stop=True)
+        def summed_product(gate, c):
+            acc = banks.tile([P, CHUNK], F32, tag="bank", name=f"acc_gate{gate}_{c}")
+            nc.tensor.matmul(acc[:], gate_block(wih_sb, gate), ctx_sb[:, chunks[c]], start=True, stop=False)
+            nc.tensor.matmul(acc[:], gate_block(whh_sb, gate), h_sb[:, chunks[c]], start=False, stop=True)
+            return acc
+
+        r = []
+        for c in range(NCHUNKS):
+            acc_r = summed_product(RESET, c)
+            r.append(held.tile([P, CHUNK], F32, name=f"r{c}"))
             nc.scalar.activation(r[c][:], acc_r[:], SIGMOID, bias=bias_rz[:, RESET : RESET + 1])
 
-        def tanh_argument(c):
+        gated = []
+        for c in range(NCHUNKS):
             acc_hc = banks.tile([P, CHUNK], F32, tag="bank", name=f"acc_hc{c}")
             nc.tensor.matmul(acc_hc[:], gate_block(whh_sb, CAND), h_sb[:, chunks[c]], start=True, stop=True)
+            gated.append(held.tile([P, CHUNK], F32, name=f"gated{c}"))
+            nc.vector.scalar_tensor_tensor(
+                gated[c][:], acc_hc[:], bhh_sb[:, CAND : CAND + 1], r[c][:], op0=ADD, op1=MULT
+            )
+
+        z = []
+        for c in range(NCHUNKS):
+            acc_z = summed_product(UPDATE, c)
+            z.append(held.tile([P, CHUNK], F32, name=f"z{c}"))
+            nc.scalar.activation(z[c][:], acc_z[:], SIGMOID, bias=bias_rz[:, UPDATE : UPDATE + 1])
+
+        tanh_arg = []
+        for c in range(NCHUNKS):
             acc_ic = banks.tile([P, CHUNK], F32, tag="bank", name=f"acc_ic{c}")
             nc.tensor.matmul(acc_ic[:], gate_block(wih_sb, CAND), ctx_sb[:, chunks[c]], start=True, stop=True)
-            gated = held.tile([P, CHUNK], F32, name=f"gated{c}")
-            nc.vector.scalar_tensor_tensor(
-                gated[:], acc_hc[:], bhh_sb[:, CAND : CAND + 1], r[c][:], op0=ADD, op1=MULT
-            )
-            nc.vector.tensor_tensor(tanh_arg[c][:], gated[:], acc_ic[:], ADD)
+            tanh_arg.append(held.tile([P, CHUNK], F32, name=f"tanh_arg{c}"))
+            nc.vector.tensor_tensor(tanh_arg[c][:], gated[c][:], acc_ic[:], ADD)
 
-        def update_gate(c, engine):
-            acc_z = banks.tile([P, CHUNK], F32, tag="bank", name=f"acc_z{c}")
-            nc.tensor.matmul(acc_z[:], gate_block(wih_sb, UPDATE), ctx_sb[:, chunks[c]], start=True, stop=False)
-            nc.tensor.matmul(acc_z[:], gate_block(whh_sb, UPDATE), h_sb[:, chunks[c]], start=False, stop=True)
-            nc.scalar.activation(z[c][:], acc_z[:], SIGMOID, bias=bias_rz[:, UPDATE : UPDATE + 1])
-            engine.tensor_tensor(kept[:, chunks[c]], z[c][:], h_sb[:, chunks[c]], MULT)
+        for c, multiplier in enumerate((nc.gpsimd, nc.vector)):
+            multiplier.tensor_tensor(kept[:, chunks[c]], z[c][:], h_sb[:, chunks[c]], MULT)
 
-        def candidate(c):
+        for c in range(NCHUNKS):
             neg_cand = held.tile([P, CHUNK], F32, name=f"neg_cand{c}")
             nc.scalar.activation(neg_cand[:], tanh_arg[c][:], TANH, bias=neg_bih_cand[:], scale=-1.0)
             nc.vector.scalar_tensor_tensor(fresh[:, chunks[c]], z[c][:], 1.0, neg_cand[:], op0=SUBTRACT, op1=MULT)
-
-        reset_gate(0)
-        tanh_argument(0)
-        reset_gate(1)
-        update_gate(0, nc.gpsimd)
-        tanh_argument(1)
-        candidate(0)
-        update_gate(1, nc.vector)
-        candidate(1)
 
         nc.vector.tensor_tensor(window[:].indirect(offsets[:]), fresh[:], kept[:], ADD)
         nc.sync.dma_start(out, window[:])

@@ -88,13 +88,11 @@ def tile_ampnn_kernel(tc, base, ctx, h, wih, whh, bih, bhh, offs, out):
             )
 
         z = []
+        tanh_arg = []
         for c in range(NCHUNKS):
             acc_z = summed_product(UPDATE, c)
             z.append(held.tile([P, CHUNK], F32, name=f"z{c}"))
             nc.scalar.activation(z[c][:], acc_z[:], SIGMOID, bias=bias_rz[:, UPDATE : UPDATE + 1])
-
-        tanh_arg = []
-        for c in range(NCHUNKS):
             acc_ic = banks.tile([P, CHUNK], F32, tag="bank", name=f"acc_ic{c}")
             nc.tensor.matmul(acc_ic[:], gate_block(wih_sb, CAND), ctx_sb[:, chunks[c]], start=True, stop=True)
             tanh_arg.append(held.tile([P, CHUNK], F32, name=f"tanh_arg{c}"))

@@ -15,6 +15,8 @@ STORE = 2048
 RESET, UPDATE, CAND = 0, 1, 2
 CHUNK = 512
 NCHUNKS = NODES // CHUNK
+BLOCK = 32
+BIAS_COLUMNS = 256
 PSUM_BANKS = 8
 WARMUP_MATMULS = 3
 
@@ -35,20 +37,24 @@ def tile_ampnn_kernel(tc, base, ctx, h, wih, whh, bih, bhh, offs, out):
         for repeat in range(WARMUP_MATMULS):
             nc.tensor.matmul(unread[:], zeros[:, 0:P], zeros[:], start=True, stop=True)
 
+        bias_rows = held.tile([P, BIAS_COLUMNS], F32, align_bytes=64, name="bias_rows")
+        nc.vector.memset(bias_rows[:], 0.0)
+
         wih_sb = held.tile([P, 3 * P], BF16, name="wih_sb")
         nc.sync.dma_start(wih_sb[:], wih)
         whh_sb = held.tile([P, 3 * P], BF16, name="whh_sb")
         nc.scalar.dma_start(whh_sb[:], whh)
         ctx_sb = held.tile([P, NODES], BF16, name="ctx_sb")
         h_sb = held.tile([P, NODES], BF16, name="h_sb")
-        for cols in chunks:
-            nc.sync.dma_start(ctx_sb[:, cols], ctx[:, cols])
-            nc.scalar.dma_start(h_sb[:, cols], h[:, cols])
-        bih_sb = held.tile([P, 3], F32, name="bih_sb")
-        bhh_sb = held.tile([P, 3], F32, name="bhh_sb")
-        with nc.allow_non_contiguous_dma(reason="384 biases, one float32 to a partition and gate"):
-            nc.sync.dma_start(bih_sb[:], bih.rearrange("(g p) o -> p (g o)", p=P))
-            nc.scalar.dma_start(bhh_sb[:], bhh.rearrange("(g p) o -> p (g o)", p=P))
+        nc.sync.dma_start(ctx_sb[:, chunks[0]], ctx[:, chunks[0]])
+        nc.scalar.dma_start(h_sb[:, chunks[0]], h[:, chunks[0]])
+        for queue, bias, first in ((nc.sync, bih, 0), (nc.scalar, bhh, 3 * BLOCK)):
+            queue.dma_start(
+                bias_rows[0:P:BLOCK, first : first + 3 * BLOCK].rearrange("q (g i) -> q g i", i=BLOCK),
+                bias.rearrange("(g q i) o -> q g (i o)", g=3, i=BLOCK),
+            )
+        nc.sync.dma_start(ctx_sb[:, chunks[1]], ctx[:, chunks[1]])
+        nc.scalar.dma_start(h_sb[:, chunks[1]], h[:, chunks[1]])
         offsets = held.tile([P, NODES // 16], U16, name="offsets")
         nc.sync.dma_start(offsets[:], offs)
         window = held.tile([P, STORE], F32, name="window")
@@ -58,10 +64,15 @@ def tile_ampnn_kernel(tc, base, ctx, h, wih, whh, bih, bhh, offs, out):
         nc.vector.memset(table_warmer[:], 0.0)
         nc.scalar.activation(table_warmer[:], table_warmer[:], SIGMOID)
 
+        bias_columns = held.tile([P, BIAS_COLUMNS], F32, align_bytes=64, name="bias_columns")
+        nc.vector.transpose(bias_columns[:], bias_rows[:])
+        bih_at = [bias_columns[:, g * BLOCK : g * BLOCK + 1] for g in range(3)]
+        bhh_at = [bias_columns[:, (3 + g) * BLOCK : (3 + g) * BLOCK + 1] for g in range(3)]
         bias_rz = held.tile([P, 2], F32, name="bias_rz")
-        nc.vector.tensor_tensor(bias_rz[:], bih_sb[:, RESET : UPDATE + 1], bhh_sb[:, RESET : UPDATE + 1], ADD)
+        for gate in (RESET, UPDATE):
+            nc.vector.tensor_tensor(bias_rz[:, gate : gate + 1], bih_at[gate], bhh_at[gate], ADD)
         neg_bih_cand = held.tile([P, 1], F32, name="neg_bih_cand")
-        nc.vector.tensor_scalar_mul(neg_bih_cand[:], bih_sb[:, CAND : CAND + 1], -1.0)
+        nc.vector.tensor_scalar_mul(neg_bih_cand[:], bih_at[CAND], -1.0)
 
         kept = held.tile([P, NODES], F32, name="kept")
         fresh = held.tile([P, NODES], F32, name="fresh")
@@ -84,7 +95,7 @@ def tile_ampnn_kernel(tc, base, ctx, h, wih, whh, bih, bhh, offs, out):
             nc.tensor.matmul(acc_hc[:], gate_block(whh_sb, CAND), h_sb[:, chunks[c]], start=True, stop=True)
             gated.append(held.tile([P, CHUNK], F32, name=f"gated{c}"))
             nc.vector.scalar_tensor_tensor(
-                gated[c][:], acc_hc[:], bhh_sb[:, CAND : CAND + 1], r[c][:], op0=ADD, op1=MULT
+                gated[c][:], acc_hc[:], bhh_at[CAND], r[c][:], op0=ADD, op1=MULT
             )
 
         z = []

@@ -16,7 +16,7 @@ RESET, UPDATE, CAND = 0, 1, 2
 CHUNK = 512
 NCHUNKS = NODES // CHUNK
 BLOCK = 32
-BIAS_COLUMNS = 256
+PAIR = 2 * BLOCK
 PSUM_BANKS = 8
 WARMUP_MATMULS = 3
 
@@ -37,7 +37,8 @@ def tile_ampnn_kernel(tc, base, ctx, h, wih, whh, bih, bhh, offs, out):
         for repeat in range(WARMUP_MATMULS):
             nc.tensor.matmul(unread[:], zeros[:, 0:P], zeros[:], start=True, stop=True)
 
-        bias_rows = held.tile([P, BIAS_COLUMNS], F32, align_bytes=64, name="bias_rows")
+        bias_rows = held.tile([P, 4 * PAIR], F32, align_bytes=64, name="bias_rows")
+        bias_row_blocks = bias_rows[0:P:BLOCK, :].rearrange("q (g s i) -> q g s i", s=2, i=BLOCK)
         nc.vector.memset(bias_rows[:], 0.0)
 
         wih_sb = held.tile([P, 3 * P], BF16, name="wih_sb")
@@ -48,10 +49,9 @@ def tile_ampnn_kernel(tc, base, ctx, h, wih, whh, bih, bhh, offs, out):
         h_sb = held.tile([P, NODES], BF16, name="h_sb")
         nc.sync.dma_start(ctx_sb[:, chunks[0]], ctx[:, chunks[0]])
         nc.scalar.dma_start(h_sb[:, chunks[0]], h[:, chunks[0]])
-        for queue, bias, first in ((nc.sync, bih, 0), (nc.scalar, bhh, 3 * BLOCK)):
+        for side, (queue, bias) in enumerate(((nc.sync, bih), (nc.scalar, bhh))):
             queue.dma_start(
-                bias_rows[0:P:BLOCK, first : first + 3 * BLOCK].rearrange("q (g i) -> q g i", i=BLOCK),
-                bias.rearrange("(g q i) o -> q g (i o)", g=3, i=BLOCK),
+                bias_row_blocks[:, 0:3, side, :], bias.rearrange("(g q i) o -> q g (i o)", g=3, i=BLOCK)
             )
         nc.sync.dma_start(ctx_sb[:, chunks[1]], ctx[:, chunks[1]])
         nc.scalar.dma_start(h_sb[:, chunks[1]], h[:, chunks[1]])
@@ -64,15 +64,15 @@ def tile_ampnn_kernel(tc, base, ctx, h, wih, whh, bih, bhh, offs, out):
         nc.vector.memset(table_warmer[:], 0.0)
         nc.scalar.activation(table_warmer[:], table_warmer[:], SIGMOID)
 
-        bias_columns = held.tile([P, BIAS_COLUMNS], F32, align_bytes=64, name="bias_columns")
-        nc.vector.transpose(bias_columns[:], bias_rows[:])
-        bih_at = [bias_columns[:, g * BLOCK : g * BLOCK + 1] for g in range(3)]
-        bhh_at = [bias_columns[:, (3 + g) * BLOCK : (3 + g) * BLOCK + 1] for g in range(3)]
+        columns_rz = held.tile([P, 2 * PAIR], F32, align_bytes=64, name="columns_rz")
+        nc.vector.transpose(columns_rz[:], bias_rows[:, 0 : 2 * PAIR])
         bias_rz = held.tile([P, 2], F32, name="bias_rz")
-        for gate in (RESET, UPDATE):
-            nc.vector.tensor_tensor(bias_rz[:, gate : gate + 1], bih_at[gate], bhh_at[gate], ADD)
+        nc.vector.tensor_tensor(bias_rz[:], columns_rz[:, 0::PAIR], columns_rz[:, BLOCK::PAIR], ADD)
+        columns_cand = held.tile([P, 2 * PAIR], F32, align_bytes=64, name="columns_cand")
+        nc.vector.transpose(columns_cand[:], bias_rows[:, 2 * PAIR : 4 * PAIR])
+        bhh_cand = columns_cand[:, BLOCK : BLOCK + 1]
         neg_bih_cand = held.tile([P, 1], F32, name="neg_bih_cand")
-        nc.vector.tensor_scalar_mul(neg_bih_cand[:], bih_at[CAND], -1.0)
+        nc.vector.tensor_scalar_mul(neg_bih_cand[:], columns_cand[:, 0:1], -1.0)
 
         kept = held.tile([P, NODES], F32, name="kept")
         fresh = held.tile([P, NODES], F32, name="fresh")
@@ -95,7 +95,7 @@ def tile_ampnn_kernel(tc, base, ctx, h, wih, whh, bih, bhh, offs, out):
             nc.tensor.matmul(acc_hc[:], gate_block(whh_sb, CAND), h_sb[:, chunks[c]], start=True, stop=True)
             gated.append(held.tile([P, CHUNK], F32, name=f"gated{c}"))
             nc.vector.scalar_tensor_tensor(
-                gated[c][:], acc_hc[:], bhh_at[CAND], r[c][:], op0=ADD, op1=MULT
+                gated[c][:], acc_hc[:], bhh_cand, r[c][:], op0=ADD, op1=MULT
             )
 
         z = []

@@ -15,6 +15,7 @@ STORE = 2048
 RESET, UPDATE, CAND = 0, 1, 2
 CHUNK = 512
 NCHUNKS = NODES // CHUNK
+HALF = CHUNK // 2
 BLOCK = 32
 PAIR = 2 * BLOCK
 PSUM_BANKS = 8
@@ -30,6 +31,7 @@ def gate_block(weights, gate):
 def tile_ampnn_kernel(tc, base, ctx, h, wih, whh, bih, bhh, offs, out):
     nc = tc.nc
     chunks = [slice(c * CHUNK, (c + 1) * CHUNK) for c in range(NCHUNKS)]
+    reset_pieces = [slice(0, HALF), slice(HALF, CHUNK), *chunks[1:]]
     with tc.tile_pool(name="held", bufs=1) as held, tc.psum_pool(name="banks", bufs=PSUM_BANKS) as banks:
         zeros = held.tile([P, CHUNK], BF16, name="zeros")
         nc.gpsimd.memset(zeros[:], 0.0)
@@ -77,37 +79,34 @@ def tile_ampnn_kernel(tc, base, ctx, h, wih, whh, bih, bhh, offs, out):
         kept = held.tile([P, NODES], F32, name="kept")
         fresh = held.tile([P, NODES], F32, name="fresh")
 
-        def summed_product(gate, c):
-            acc = banks.tile([P, CHUNK], F32, tag="bank", name=f"acc_gate{gate}_{c}")
-            nc.tensor.matmul(acc[:], gate_block(wih_sb, gate), ctx_sb[:, chunks[c]], start=True, stop=False)
-            nc.tensor.matmul(acc[:], gate_block(whh_sb, gate), h_sb[:, chunks[c]], start=False, stop=True)
+        def summed_product(gate, nodes):
+            bank = banks.tile([P, CHUNK], F32, tag="bank", name=f"acc_gate{gate}_{nodes.start}")
+            acc = bank[:, 0 : nodes.stop - nodes.start]
+            nc.tensor.matmul(acc, gate_block(wih_sb, gate), ctx_sb[:, nodes], start=True, stop=False)
+            nc.tensor.matmul(acc, gate_block(whh_sb, gate), h_sb[:, nodes], start=False, stop=True)
             return acc
 
-        r = []
-        for c in range(NCHUNKS):
-            acc_r = summed_product(RESET, c)
-            r.append(held.tile([P, CHUNK], F32, name=f"r{c}"))
-            nc.scalar.activation(r[c][:], acc_r[:], SIGMOID, bias=bias_rz[:, RESET : RESET + 1])
-
-        gated = []
-        for c in range(NCHUNKS):
-            acc_hc = banks.tile([P, CHUNK], F32, tag="bank", name=f"acc_hc{c}")
-            nc.tensor.matmul(acc_hc[:], gate_block(whh_sb, CAND), h_sb[:, chunks[c]], start=True, stop=True)
-            gated.append(held.tile([P, CHUNK], F32, name=f"gated{c}"))
-            nc.vector.scalar_tensor_tensor(
-                gated[c][:], acc_hc[:], bhh_cand, r[c][:], op0=ADD, op1=MULT
+        r = held.tile([P, NODES], F32, name="r")
+        gated = held.tile([P, NODES], F32, name="gated")
+        for nodes in reset_pieces:
+            nc.scalar.activation(
+                r[:, nodes], summed_product(RESET, nodes), SIGMOID, bias=bias_rz[:, RESET : RESET + 1]
             )
+            bank = banks.tile([P, CHUNK], F32, tag="bank", name=f"acc_hc{nodes.start}")
+            acc_hc = bank[:, 0 : nodes.stop - nodes.start]
+            nc.tensor.matmul(acc_hc, gate_block(whh_sb, CAND), h_sb[:, nodes], start=True, stop=True)
+            nc.vector.scalar_tensor_tensor(gated[:, nodes], acc_hc, bhh_cand, r[:, nodes], op0=ADD, op1=MULT)
 
         z = []
         tanh_arg = []
         for c in range(NCHUNKS):
-            acc_z = summed_product(UPDATE, c)
+            acc_z = summed_product(UPDATE, chunks[c])
             z.append(held.tile([P, CHUNK], F32, name=f"z{c}"))
-            nc.scalar.activation(z[c][:], acc_z[:], SIGMOID, bias=bias_rz[:, UPDATE : UPDATE + 1])
+            nc.scalar.activation(z[c][:], acc_z, SIGMOID, bias=bias_rz[:, UPDATE : UPDATE + 1])
             acc_ic = banks.tile([P, CHUNK], F32, tag="bank", name=f"acc_ic{c}")
             nc.tensor.matmul(acc_ic[:], gate_block(wih_sb, CAND), ctx_sb[:, chunks[c]], start=True, stop=True)
             tanh_arg.append(held.tile([P, CHUNK], F32, name=f"tanh_arg{c}"))
-            nc.vector.tensor_tensor(tanh_arg[c][:], gated[c][:], acc_ic[:], ADD)
+            nc.vector.tensor_tensor(tanh_arg[c][:], gated[:, chunks[c]], acc_ic[:], ADD)
 
         for c, multiplier in enumerate((nc.gpsimd, nc.vector)):
             multiplier.tensor_tensor(kept[:, chunks[c]], z[c][:], h_sb[:, chunks[c]], MULT)

@@ -19,7 +19,7 @@ HALF = CHUNK // 2
 BLOCK = 32
 PAIR = 2 * BLOCK
 PSUM_BANKS = 8
-WARMUP_MATMULS = 3
+WARMUP_MATMULS = 16
 
 FLOPS = 2 * 2 * P * 3 * P * NODES
 
@@ -33,11 +33,11 @@ def tile_ampnn_kernel(tc, base, ctx, h, wih, whh, bih, bhh, offs, out):
     chunks = [slice(c * CHUNK, (c + 1) * CHUNK) for c in range(NCHUNKS)]
     reset_pieces = [slice(0, HALF), slice(HALF, CHUNK), *chunks[1:]]
     with tc.tile_pool(name="held", bufs=1) as held, tc.psum_pool(name="banks", bufs=PSUM_BANKS) as banks:
-        zeros = held.tile([P, CHUNK], BF16, name="zeros")
+        zeros = held.tile([P, P], BF16, name="zeros")
         nc.gpsimd.memset(zeros[:], 0.0)
         unread = banks.tile([P, CHUNK], F32, tag="bank", name="unread")
         for repeat in range(WARMUP_MATMULS):
-            nc.tensor.matmul(unread[:], zeros[:, 0:P], zeros[:], start=True, stop=True)
+            nc.tensor.matmul(unread[:, 0:P], zeros[:], zeros[:], start=True, stop=True)
 
         bias_rows = held.tile([P, 4 * PAIR], F32, align_bytes=64, name="bias_rows")
         bias_row_blocks = bias_rows[0:P:BLOCK, :].rearrange("q (g s i) -> q g s i", s=2, i=BLOCK)

import concourse.mybir as mybir

F32 = mybir.dt.float32
BF16 = mybir.dt.bfloat16
U16 = mybir.dt.uint16
ADD = mybir.AluOpType.add
SUBTRACT = mybir.AluOpType.subtract
MULT = mybir.AluOpType.mult
SIGMOID = mybir.ActivationFunctionType.Sigmoid
TANH = mybir.ActivationFunctionType.Tanh

P = 128
NODES = 1024
STORE = 2048
RESET, UPDATE, CAND = 0, 1, 2
CHUNK = 512
NCHUNKS = NODES // CHUNK
HALF = CHUNK // 2
BLOCK = 32
PAIR = 2 * BLOCK
PSUM_BANKS = 8
WARMUP_MATMULS = 16

FLOPS = 2 * 2 * P * 3 * P * NODES


def gate_block(weights, gate):
    return weights[:, gate * P : (gate + 1) * P]


def tile_ampnn_kernel(tc, base, ctx, h, wih, whh, bih, bhh, offs, out):
    nc = tc.nc
    chunks = [slice(c * CHUNK, (c + 1) * CHUNK) for c in range(NCHUNKS)]
    reset_pieces = [slice(0, HALF), slice(HALF, CHUNK), *chunks[1:]]
    with tc.tile_pool(name="held", bufs=1) as held, tc.psum_pool(name="banks", bufs=PSUM_BANKS) as banks:
        zeros = held.tile([P, P], BF16, name="zeros")
        nc.gpsimd.memset(zeros[:], 0.0)
        unread = banks.tile([P, CHUNK], F32, tag="bank", name="unread")
        for repeat in range(WARMUP_MATMULS):
            nc.tensor.matmul(unread[:, 0:P], zeros[:], zeros[:], start=True, stop=True)

        bias_rows = held.tile([P, 4 * PAIR], F32, align_bytes=64, name="bias_rows")
        bias_row_blocks = bias_rows[0:P:BLOCK, :].rearrange("q (g s i) -> q g s i", s=2, i=BLOCK)
        nc.vector.memset(bias_rows[:], 0.0)

        wih_sb = held.tile([P, 3 * P], BF16, name="wih_sb")
        nc.sync.dma_start(wih_sb[:], wih)
        whh_sb = held.tile([P, 3 * P], BF16, name="whh_sb")
        nc.scalar.dma_start(whh_sb[:], whh)
        ctx_sb = held.tile([P, NODES], BF16, name="ctx_sb")
        h_sb = held.tile([P, NODES], BF16, name="h_sb")
        nc.sync.dma_start(ctx_sb[:, chunks[0]], ctx[:, chunks[0]])
        nc.scalar.dma_start(h_sb[:, chunks[0]], h[:, chunks[0]])
        for side, (queue, bias) in enumerate(((nc.sync, bih), (nc.scalar, bhh))):
            queue.dma_start(
                bias_row_blocks[:, 0:3, side, :], bias.rearrange("(g q i) o -> q g (i o)", g=3, i=BLOCK)
            )
        nc.sync.dma_start(ctx_sb[:, chunks[1]], ctx[:, chunks[1]])
        nc.scalar.dma_start(h_sb[:, chunks[1]], h[:, chunks[1]])
        offsets = held.tile([P, NODES // 16], U16, name="offsets")
        nc.sync.dma_start(offsets[:], offs)
        window = held.tile([P, STORE], F32, name="window")
        nc.sync.dma_start(window[:], base)

        table_warmer = held.tile([P, 1], F32, name="table_warmer")
        nc.vector.memset(table_warmer[:], 0.0)
        nc.scalar.activation(table_warmer[:], table_warmer[:], SIGMOID)

        columns_rz = held.tile([P, 2 * PAIR], F32, align_bytes=64, name="columns_rz")
        nc.vector.transpose(columns_rz[:], bias_rows[:, 0 : 2 * PAIR])
        bias_rz = held.tile([P, 2], F32, name="bias_rz")
        nc.vector.tensor_tensor(bias_rz[:], columns_rz[:, 0::PAIR], columns_rz[:, BLOCK::PAIR], ADD)
        columns_cand = held.tile([P, 2 * PAIR], F32, align_bytes=64, name="columns_cand")
        nc.vector.transpose(columns_cand[:], bias_rows[:, 2 * PAIR : 4 * PAIR])
        bhh_cand = columns_cand[:, BLOCK : BLOCK + 1]
        neg_bih_cand = held.tile([P, 1], F32, name="neg_bih_cand")
        nc.vector.tensor_scalar_mul(neg_bih_cand[:], columns_cand[:, 0:1], -1.0)

        kept = held.tile([P, NODES], F32, name="kept")
        fresh = held.tile([P, NODES], F32, name="fresh")

        def summed_product(gate, nodes):
            bank = banks.tile([P, CHUNK], F32, tag="bank", name=f"acc_gate{gate}_{nodes.start}")
            acc = bank[:, 0 : nodes.stop - nodes.start]
            nc.tensor.matmul(acc, gate_block(wih_sb, gate), ctx_sb[:, nodes], start=True, stop=False)
            nc.tensor.matmul(acc, gate_block(whh_sb, gate), h_sb[:, nodes], start=False, stop=True)
            return acc

        r = held.tile([P, NODES], F32, name="r")
        gated = held.tile([P, NODES], F32, name="gated")
        for nodes in reset_pieces:
            nc.scalar.activation(
                r[:, nodes], summed_product(RESET, nodes), SIGMOID, bias=bias_rz[:, RESET : RESET + 1]
            )
            bank = banks.tile([P, CHUNK], F32, tag="bank", name=f"acc_hc{nodes.start}")
            acc_hc = bank[:, 0 : nodes.stop - nodes.start]
            nc.tensor.matmul(acc_hc, gate_block(whh_sb, CAND), h_sb[:, nodes], start=True, stop=True)
            nc.vector.scalar_tensor_tensor(gated[:, nodes], acc_hc, bhh_cand, r[:, nodes], op0=ADD, op1=MULT)

        z = []
        tanh_arg = []
        for c in range(NCHUNKS):
            acc_z = summed_product(UPDATE, chunks[c])
            z.append(held.tile([P, CHUNK], F32, name=f"z{c}"))
            nc.scalar.activation(z[c][:], acc_z, SIGMOID, bias=bias_rz[:, UPDATE : UPDATE + 1])
            acc_ic = banks.tile([P, CHUNK], F32, tag="bank", name=f"acc_ic{c}")
            nc.tensor.matmul(acc_ic[:], gate_block(wih_sb, CAND), ctx_sb[:, chunks[c]], start=True, stop=True)
            tanh_arg.append(held.tile([P, CHUNK], F32, name=f"tanh_arg{c}"))
            nc.vector.tensor_tensor(tanh_arg[c][:], gated[:, chunks[c]], acc_ic[:], ADD)

        for c, multiplier in enumerate((nc.gpsimd, nc.vector)):
            multiplier.tensor_tensor(kept[:, chunks[c]], z[c][:], h_sb[:, chunks[c]], MULT)

        for c in range(NCHUNKS):
            neg_cand = held.tile([P, CHUNK], F32, name=f"neg_cand{c}")
            nc.scalar.activation(neg_cand[:], tanh_arg[c][:], TANH, bias=neg_bih_cand[:], scale=-1.0)
            nc.vector.scalar_tensor_tensor(fresh[:, chunks[c]], z[c][:], 1.0, neg_cand[:], op0=SUBTRACT, op1=MULT)

        nc.vector.tensor_tensor(window[:].indirect(offsets[:]), fresh[:], kept[:], ADD)
        nc.sync.dma_start(out, window[:])
